import numpy as np
import ml_dtypes


def mxq(x, axis, fmt="e4m3"):
    dtype, down = {"e4m3": (ml_dtypes.float8_e4m3fn, 7), "e5m2": (ml_dtypes.float8_e5m2, 14)}[fmt]
    v = np.moveaxis(np.asarray(x, np.float32).astype(ml_dtypes.bfloat16).astype(np.float64), axis, -1)
    blocks = v.reshape(v.shape[:-1] + (-1, 32))
    amax = np.abs(blocks).max(-1, keepdims=True)
    byte = np.maximum(np.where(amax > 0, np.frexp(amax)[1] - 1 + 127, 0) - down, 1)
    scale = np.exp2(byte - 127.0)
    codes = (blocks / scale).astype(np.float32).astype(dtype).astype(np.float64)
    return np.moveaxis((codes * scale).reshape(v.shape), -1, axis)


WIDE = False


def mx_kscale(k):
    if not WIDE:
        return np.ones(k)
    levels = np.array([10, -10, 5, -5, 0])
    a = np.random.permutation(np.resize(levels, k // 512 * 4)).reshape(k // 512, 4)
    idx = np.arange(k)
    return np.exp2(a[idx // 512, idx % 128 // 32])


BF16 = ml_dtypes.bfloat16


def bf(x):
    return np.asarray(x, np.float32).astype(BF16)


def f64(x):
    return np.asarray(x).astype(np.float64)


E2M1 = np.array([0.0, 0.5, 1.0, 1.5, 2.0, 3.0, 4.0, 6.0, -0.0, -0.5, -1.0, -1.5, -2.0, -3.0, -4.0, -6.0])


def pack_weight(w, fmt):
    k, n = w.shape
    w = f64(bf(w)).reshape(k // 32, 32, n)
    amax = np.abs(w).max(1)
    if fmt == "e4m3":
        byte = np.frexp(amax)[1] - 1 + 127 - 7
    else:
        mant, ex = np.frexp(amax / 6.0)
        byte = np.where(mant > 0.5, ex, ex - 1) + 127
    byte = np.clip(np.where(amax > 0, byte, 1), 1, 254)
    scaled = (w * np.exp2(127.0 - byte)[:, None, :]).reshape(k, n).astype(np.float32)
    by_word = np.ascontiguousarray(scaled.reshape(k // 512, 128, 4, n).transpose(0, 1, 3, 2))
    if fmt == "e4m3":
        words = by_word.astype(ml_dtypes.float8_e4m3fn).view(np.uint8)
    else:
        c = by_word.astype(ml_dtypes.float4_e2m1fn).view(np.uint8) & 0xF
        words = c[..., 0::2] | (c[..., 1::2] << 4)
    return np.ascontiguousarray(words), np.ascontiguousarray(byte.astype(np.uint8).reshape(k // 512, 16, n))


def unpack_weight(words, scales, fmt):
    g, p, n, _ = words.shape
    if fmt == "e4m3":
        vals = np.ascontiguousarray(words).view(ml_dtypes.float8_e4m3fn).astype(np.float64)
    else:
        nib = np.empty((g, p, n, 4), np.uint8)
        nib[..., 0::2] = words & 0xF
        nib[..., 1::2] = words >> 4
        vals = E2M1[nib]
    vals = vals * np.repeat(np.exp2(scales.astype(np.float64) - 127.0), 8, axis=1)[..., None]
    return vals.transpose(0, 1, 3, 2).reshape(g * 512, n)


BQ, BK, L, H, DH = 64, 4, 128, 4, 128
D = H * DH
FMT = "e4m3"


def setup_inputs():
    s, t = mx_kscale(D), mx_kscale(D)
    amp_q = 0.5 + np.random.random((BQ, 1, 1))
    amp_k = 0.5 + np.random.random((BK, 1, 1))
    query_states = bf(np.random.standard_normal((BQ, L, D)) * amp_q * s)
    key_states = bf(np.random.standard_normal((BK, L, D)) * amp_k * s)
    Wq = np.random.standard_normal((D, D)) * 0.8 / np.sqrt(D) * t[:, None] / s[None, :]
    bq = bf(np.random.standard_normal(D) * 0.3 * t)
    Wk = np.random.standard_normal((D, D)) * 0.8 / np.sqrt(D) / t[:, None] / s[None, :]
    bk = bf(np.random.standard_normal(D) * 0.3 / t)
    logit_scale = bf(-1.5 + 0.1 * np.random.standard_normal(1))
    Wq_words, Wq_scales = pack_weight(np.ascontiguousarray(Wq.T), FMT)
    Wk_words, Wk_scales = pack_weight(np.ascontiguousarray(Wk.T), FMT)
    return {
        "query_states": query_states,
        "key_states": key_states,
        "Wq_words": Wq_words,
        "Wq_scales": Wq_scales,
        "bq": bq,
        "Wk_words": Wk_words,
        "Wk_scales": Wk_scales,
        "bk": bk,
        "logit_scale": logit_scale,
    }


def reference(query_states, key_states, Wq_words, Wq_scales, bq, Wk_words, Wk_scales, bk, logit_scale):
    q = (mxq(f64(query_states).reshape(BQ * L, D), 1, "e4m3") @ unpack_weight(Wq_words, Wq_scales, FMT)) + f64(bq)
    k = (mxq(f64(key_states).reshape(BK * L, D), 1, "e4m3") @ unpack_weight(Wk_words, Wk_scales, FMT)) + f64(bk)
    retrieve = mxq(q, 1, "e4m3") @ mxq(k, 1, "e4m3").T
    retrieve = retrieve.reshape(BQ, L, BK, L).transpose(0, 2, 1, 3)
    t2v = retrieve.max(axis=-1).sum(axis=2) / L
    v2t = retrieve.max(axis=-2).sum(axis=2) / L
    return np.exp(f64(logit_scale)) * (t2v + v2t) / 2.0

@@ -1,0 +1,248 @@
+from contextlib import ExitStack
+
+import concourse.mybir as mybir
+from concourse.masks import make_identity
+
+F32 = mybir.dt.float32
+BF16 = mybir.dt.bfloat16
+I32 = mybir.dt.int32
+U32 = mybir.dt.uint32
+U8 = mybir.dt.uint8
+FP8X4 = mybir.dt.float8_e4m3fn_x4
+ACT = mybir.ActivationFunctionType
+ALU = mybir.AluOpType
+AXIS_X = mybir.AxisListType.X
+
+P = 128
+PACK = 4
+D = P * PACK
+N_QUERY = 64
+N_KEY = 4
+GROUP = 4
+TOKENS = GROUP * P
+N_STEPS = N_QUERY // GROUP
+REGROUP_PIECES = 2
+N_GROUPS = N_STEPS + 1
+
+FLOPS = 2 * (N_QUERY + N_KEY) * P * D * D + 2 * N_QUERY * P * N_KEY * P * D
+
+
+def tile_attention_pa_t_kernel(
+    tc, query_states, key_states, Wq_words, Wq_scales, bq, Wk_words, Wk_scales, bk, logit_scale, out
+):
+    nc = tc.nc
+    with ExitStack() as stack:
+        consts = stack.enter_context(tc.tile_pool(name="consts", bufs=1))
+        loads = stack.enter_context(tc.tile_pool(name="loads", bufs=1))
+        work = stack.enter_context(tc.tile_pool(name="work", bufs=2))
+        single = stack.enter_context(tc.tile_pool(name="single", bufs=1))
+        psum_x = stack.enter_context(tc.psum_pool(name="psum_x", bufs=2))
+        psum_q = stack.enter_context(tc.psum_pool(name="psum_q", bufs=2))
+        psum_r = stack.enter_context(tc.psum_pool(name="psum_r", bufs=4))
+        stack.enter_context(tc.manual_schedule())
+
+        w_scales = consts.tile([P, 2, D], U8, align_bytes=64)
+        nc.vector.memset(w_scales[:].rearrange("p w n -> p (w n)").bitcast(I32), 0)
+        bias_rows = consts.tile([P, P], BF16)
+        nc.vector.memset(bias_rows[:], 0.0)
+        mean_weights = consts.tile([P, P], F32)
+        nc.vector.memset(mean_weights[:], 1.0 / (2 * P))
+        identity = consts.tile([P, P], F32)
+        make_identity(nc, identity[:])
+
+        x_tiles = {}
+        w_words = consts.tile([P, 2, D], U32, align_bytes=64)
+
+        def load_x(g):
+            for s in range(GROUP):
+                x_tiles[g, s] = loads.tile([P, D], BF16, name="x_%d_%d" % (g, s))
+                sample = key_states[s] if g == 0 else query_states[GROUP * (g - 1) + s]
+                nc.sync.dma_start(out=x_tiles[g, s][:], in_=sample)
+
+        def load_weight(w, words, scales):
+            for quadrant in range(4):
+                nc.sync.dma_start(
+                    out=w_scales[32 * quadrant : 32 * quadrant + 4, w, :].bitcast(I32),
+                    in_=scales[0, 4 * quadrant : 4 * quadrant + 4, :].bitcast(I32),
+                )
+            nc.sync.dma_start(
+                out=w_words[:, w, :].bitcast(I32),
+                in_=words[0].rearrange("p n t -> p (n t)").bitcast(I32),
+            )
+
+        load_x(0)
+        load_weight(0, Wk_words, Wk_scales)
+        load_x(1)
+        load_weight(1, Wq_words, Wq_scales)
+        for g in range(2, N_GROUPS):
+            load_x(g)
+
+        nc.scalar.dma_start(out=bias_rows[0:PACK, :], in_=bk.rearrange("(j p) -> j p", p=P))
+        nc.scalar.dma_start(out=bias_rows[PACK : 2 * PACK, :], in_=bq.rearrange("(j p) -> j p", p=P))
+        log_gain = consts.tile([P, 1], BF16)
+        nc.scalar.dma_start(out=log_gain[:], in_=logit_scale.partition_broadcast(P))
+        gain = consts.tile([P, 1], F32)
+        nc.scalar.activation(out=gain[:], in_=log_gain[:], func=ACT.Exp)
+
+        bias_rows_f32 = consts.tile([P, P], F32)
+        nc.vector.tensor_copy(out=bias_rows_f32[:], in_=bias_rows[:])
+        bias_t = psum_x.tile([P, 2, 2 * P], F32, tag="xt")
+        nc.tensor.transpose(bias_t[:, 0, 0:P], bias_rows_f32[:], identity[:])
+        bias = consts.tile([P, 2 * PACK], F32)
+        nc.vector.tensor_copy(out=bias[:], in_=bias_t[:, 0, 0 : 2 * PACK])
+
+        k_codes = consts.tile([P, TOKENS], U32, align_bytes=64)
+        k_scales = consts.tile([P, TOKENS], U8, align_bytes=64)
+        row_max = consts.tile([P, N_QUERY, N_KEY], F32)
+        col_max = consts.tile([P, N_KEY, N_QUERY], F32)
+
+        x_grouped = {}
+        x_codes = {}
+        x_scales = {}
+        q_planes = {}
+        q_grouped = {}
+        q_codes = {0: k_codes}
+        q_scales = {0: k_scales}
+
+        def transpose_x(g):
+            x_grouped[g] = work.tile([P, TOKENS, PACK], BF16, name="x_grouped", align_bytes=64)
+            words_out = x_grouped[g][:].rearrange("p t c -> p (t c)").bitcast(F32).rearrange("p (t u) -> p t u", u=2)
+            for half in range(2):
+                xt = psum_x.tile([P, 2, 2 * P], F32, tag="xt")
+                for s in range(2):
+                    words_in = x_tiles[g, 2 * half + s][:].bitcast(F32)
+                    for u in range(2):
+                        nc.tensor.transpose(xt[:, u, P * s : P * (s + 1)], words_in[:, u : D // 2 : 2], identity[:])
+                nc.scalar.copy(
+                    out=words_out[:, 2 * P * half : 2 * P * (half + 1), :],
+                    in_=xt[:].rearrange("p u t -> p t u"),
+                )
+
+        def quantise_x(g):
+            x_codes[g] = work.tile([P, TOKENS], U32, name="x_codes", align_bytes=64)
+            x_scales[g] = work.tile([P, TOKENS], U8, name="x_scales", align_bytes=64)
+            nc.vector.quantize_mx(
+                out=x_codes[g][:].bitcast(FP8X4),
+                scales=x_scales[g][:],
+                in_=x_grouped[g][:].rearrange("p t c -> p (t c)"),
+            )
+
+        def project(g):
+            w = 0 if g == 0 else 1
+            q_planes[g] = work.tile([P, PACK, TOKENS], BF16, name="q_planes")
+            for j in range(PACK):
+                acc = psum_q.tile([P, TOKENS], F32, tag="acc")
+                nc.tensor.matmul_mx(
+                    out=acc[:],
+                    lhsT=w_words[:, w, P * j : P * (j + 1)].bitcast(FP8X4),
+                    lhsT_scale=w_scales[:, w, P * j : P * (j + 1)],
+                    rhs=x_codes[g][:].bitcast(FP8X4),
+                    rhs_scale=x_scales[g][:],
+                    start=True,
+                    stop=True,
+                )
+                nc.scalar.activation(
+                    out=q_planes[g][:, j, :],
+                    in_=acc[:],
+                    func=ACT.Identity,
+                    bias=bias[:, PACK * w + j : PACK * w + j + 1],
+                    scale=1.0,
+                )
+
+        def regroup(g):
+            q_grouped[g] = single.tile([P, TOKENS, PACK], BF16, name="q_grouped", align_bytes=64)
+            piece = TOKENS // REGROUP_PIECES
+            for i in range(REGROUP_PIECES):
+                nc.gpsimd.tensor_scalar(
+                    out=q_grouped[g][:, piece * i : piece * (i + 1), :],
+                    in0=q_planes[g][:, :, piece * i : piece * (i + 1)].rearrange("p j t -> p t j"),
+                    scalar1=1.0,
+                    scalar2=0.0,
+                    op0=ALU.mult,
+                    op1=ALU.add,
+                )
+
+        def quantise_q(g):
+            if g > 0:
+                q_codes[g] = work.tile([P, TOKENS], U32, name="q_codes", align_bytes=64)
+                q_scales[g] = work.tile([P, TOKENS], U8, name="q_scales", align_bytes=64)
+            nc.vector.quantize_mx(
+                out=q_codes[g][:].bitcast(FP8X4),
+                scales=q_scales[g][:],
+                in_=q_grouped[g][:].rearrange("p t c -> p (t c)"),
+            )
+
+        banks = {}
+
+        def pass_by_query_token(g, s):
+            r = psum_r.tile([P, N_KEY, P], F32, tag="r")
+            nc.tensor.matmul_mx(
+                out=r[:].rearrange("l b m -> l (b m)"),
+                lhsT=q_codes[g][:, P * s : P * (s + 1)].bitcast(FP8X4),
+                lhsT_scale=q_scales[g][:, P * s : P * (s + 1)],
+                rhs=k_codes[:].bitcast(FP8X4),
+                rhs_scale=k_scales[:],
+                start=True,
+                stop=True,
+            )
+            banks["query", g, s] = r
+
+        def max_by_query_token(g, s):
+            nc.vector.tensor_reduce(
+                out=row_max[:, GROUP * (g - 1) + s, :], in_=banks["query", g, s][:], axis=AXIS_X, op=ALU.max
+            )
+
+        def pass_by_key_token(g, b):
+            r = psum_r.tile([P, GROUP, P], F32, tag="r")
+            nc.tensor.matmul_mx(
+                out=r[:].rearrange("m a l -> m (a l)"),
+                lhsT=k_codes[:, P * b : P * (b + 1)].bitcast(FP8X4),
+                lhsT_scale=k_scales[:, P * b : P * (b + 1)],
+                rhs=q_codes[g][:].bitcast(FP8X4),
+                rhs_scale=q_scales[g][:],
+                start=True,
+                stop=True,
+            )
+            banks["key", g, b] = r
+
+        def max_by_key_token(g, b):
+            nc.vector.tensor_reduce(
+                out=col_max[:, b, GROUP * (g - 1) : GROUP * g], in_=banks["key", g, b][:], axis=AXIS_X, op=ALU.max
+            )
+
+        def when_valid(stage, g):
+            if 0 <= g < N_GROUPS:
+                stage(g)
+
+        for g in range(-4, N_GROUPS):
+            if g >= 1:
+                for i in range(4):
+                    max_by_query_token(g, i)
+                    pass_by_key_token(g, i)
+            when_valid(quantise_x, g + 3)
+            when_valid(quantise_q, g + 1)
+            when_valid(transpose_x, g + 4)
+            when_valid(regroup, g + 2)
+            for i in range(4):
+                if g >= 1:
+                    max_by_key_token(g, i)
+                if 1 <= g + 1 < N_GROUPS:
+                    pass_by_query_token(g + 1, i)
+            when_valid(project, g + 3)
+
+        both_max = consts.tile([P, N_QUERY, N_KEY], F32)
+        nc.vector.tensor_tensor(
+            out=both_max[:], in0=row_max[:], in1=col_max[:].rearrange("p b a -> p a b"), op=ALU.add
+        )
+        means = psum_r.tile([P, N_KEY, P], F32, tag="r")
+        means_flat = means[:].rearrange("p b m -> p (b m)")[:, 0 : N_QUERY * N_KEY]
+        nc.tensor.matmul(
+            out=means_flat,
+            lhsT=mean_weights[:],
+            rhs=both_max[:].rearrange("p a b -> p (a b)"),
+            start=True,
+            stop=True,
+        )
+        result = consts.tile([P, N_QUERY * N_KEY], F32)
+        nc.scalar.activation(out=result[:], in_=means_flat, func=ACT.Copy, scale=gain[:, 0:1])
+        nc.sync.dma_start(out=out.rearrange("a b -> (a b)").unsqueeze(0), in_=result[0:1, :])

@@ -22,6 +22,7 @@ GROUP = 4
 TOKENS = GROUP * P
 N_STEPS = N_QUERY // GROUP
 REGROUP_PIECES = 2
+HEAD_GROUPS = 2
 N_GROUPS = N_STEPS + 1
 
 FLOPS = 2 * (N_QUERY + N_KEY) * P * D * D + 2 * N_QUERY * P * N_KEY * P * D
@@ -81,20 +82,20 @@ def tile_attention_pa_t_kernel(
         nc.scalar.dma_start(out=bias_rows[PACK : 2 * PACK, :], in_=bq.rearrange("(j p) -> j p", p=P))
         log_gain = consts.tile([P, 1], BF16)
         nc.scalar.dma_start(out=log_gain[:], in_=logit_scale.partition_broadcast(P))
-        gain = consts.tile([P, 1], F32)
-        nc.scalar.activation(out=gain[:], in_=log_gain[:], func=ACT.Exp)
 
-        bias_rows_f32 = consts.tile([P, P], F32)
-        nc.vector.tensor_copy(out=bias_rows_f32[:], in_=bias_rows[:])
-        bias_t = psum_x.tile([P, 2, 2 * P], F32, tag="xt")
-        nc.tensor.transpose(bias_t[:, 0, 0:P], bias_rows_f32[:], identity[:])
         bias = consts.tile([P, 2 * PACK], F32)
-        nc.vector.tensor_copy(out=bias[:], in_=bias_t[:, 0, 0 : 2 * PACK])
+
+        def spread_biases():
+            bias_rows_f32 = consts.tile([P, P], F32)
+            nc.vector.tensor_copy(out=bias_rows_f32[:], in_=bias_rows[:])
+            bias_t = psum_q.tile([P, TOKENS], F32, tag="acc")
+            nc.tensor.transpose(bias_t[:, 0:P], bias_rows_f32[:], identity[:])
+            nc.vector.tensor_copy(out=bias[:], in_=bias_t[:, 0 : 2 * PACK])
 
         k_codes = consts.tile([P, TOKENS], U32, align_bytes=64)
         k_scales = consts.tile([P, TOKENS], U8, align_bytes=64)
         row_max = consts.tile([P, N_QUERY, N_KEY], F32)
-        col_max = consts.tile([P, N_KEY, N_QUERY], F32)
+        col_max = consts.tile([P, N_QUERY, N_KEY], F32)
 
         x_grouped = {}
         x_codes = {}
@@ -151,6 +152,12 @@ def tile_attention_pa_t_kernel(
 
         def regroup(g):
             q_grouped[g] = single.tile([P, TOKENS, PACK], BF16, name="q_grouped", align_bytes=64)
+            if g < HEAD_GROUPS:
+                nc.vector.tensor_copy(
+                    out=q_grouped[g][:].rearrange("p (c i) j -> p c j i", i=4),
+                    in_=q_planes[g][:].rearrange("p j (c i) -> p c j i", i=4),
+                )
+                return
             piece = TOKENS // REGROUP_PIECES
             for i in range(REGROUP_PIECES):
                 nc.gpsimd.tensor_scalar(
@@ -207,7 +214,7 @@ def tile_attention_pa_t_kernel(
 
         def max_by_key_token(g, b):
             nc.vector.tensor_reduce(
-                out=col_max[:, b, GROUP * (g - 1) : GROUP * g], in_=banks["key", g, b][:], axis=AXIS_X, op=ALU.max
+                out=col_max[:, GROUP * (g - 1) : GROUP * g, b], in_=banks["key", g, b][:], axis=AXIS_X, op=ALU.max
             )
 
         def when_valid(stage, g):
@@ -215,6 +222,8 @@ def tile_attention_pa_t_kernel(
                 stage(g)
 
         for g in range(-4, N_GROUPS):
+            if g == -3:
+                spread_biases()
             if g >= 1:
                 for i in range(4):
                     max_by_query_token(g, i)
@@ -230,18 +239,15 @@ def tile_attention_pa_t_kernel(
                     pass_by_query_token(g + 1, i)
             when_valid(project, g + 3)
 
-        both_max = consts.tile([P, N_QUERY, N_KEY], F32)
-        nc.vector.tensor_tensor(
-            out=both_max[:], in0=row_max[:], in1=col_max[:].rearrange("p b a -> p a b"), op=ALU.add
-        )
-        means = psum_r.tile([P, N_KEY, P], F32, tag="r")
-        means_flat = means[:].rearrange("p b m -> p (b m)")[:, 0 : N_QUERY * N_KEY]
+        gain = consts.tile([P, 1], F32)
+        nc.scalar.activation(out=gain[:], in_=log_gain[:], func=ACT.Exp)
+        means = psum_q.tile([P, TOKENS], F32, tag="acc")
+        means_flat = means[:, 0 : N_QUERY * N_KEY]
         nc.tensor.matmul(
-            out=means_flat,
-            lhsT=mean_weights[:],
-            rhs=both_max[:].rearrange("p a b -> p (a b)"),
-            start=True,
-            stop=True,
+            out=means_flat, lhsT=mean_weights[:], rhs=row_max[:].rearrange("p a b -> p (a b)"), start=True, stop=False
+        )
+        nc.tensor.matmul(
+            out=means_flat, lhsT=mean_weights[:], rhs=col_max[:].rearrange("p a b -> p (a b)"), start=False, stop=True
         )
         result = consts.tile([P, N_QUERY * N_KEY], F32)
         nc.scalar.activation(out=result[:], in_=means_flat, func=ACT.Copy, scale=gain[:, 0:1])

@@ -20,9 +20,9 @@ N_QUERY = 64
 N_KEY = 4
 GROUP = 4
 TOKENS = GROUP * P
+HALF = TOKENS // 2
 N_STEPS = N_QUERY // GROUP
 REGROUP_PIECES = 2
-HEAD_GROUPS = 2
 N_GROUPS = N_STEPS + 1
 
 FLOPS = 2 * (N_QUERY + N_KEY) * P * D * D + 2 * N_QUERY * P * N_KEY * P * D
@@ -44,8 +44,9 @@ def tile_attention_pa_t_kernel(
 
         w_scales = consts.tile([P, 2, D], U8, align_bytes=64)
         nc.vector.memset(w_scales[:].rearrange("p w n -> p (w n)").bitcast(I32), 0)
-        bias_rows = consts.tile([P, P], BF16)
-        nc.vector.memset(bias_rows[:], 0.0)
+        bias_rows = [consts.tile([P, P], BF16, name="bias_rows_%d" % w) for w in range(2)]
+        for w in range(2):
+            nc.vector.memset(bias_rows[w][:], 0.0)
         mean_weights = consts.tile([P, P], F32)
         nc.vector.memset(mean_weights[:], 1.0 / (2 * P))
         identity = consts.tile([P, P], F32)
@@ -54,43 +55,54 @@ def tile_attention_pa_t_kernel(
         x_tiles = {}
         w_words = consts.tile([P, 2, D], U32, align_bytes=64)
 
-        def load_x(g):
-            for s in range(GROUP):
-                x_tiles[g, s] = loads.tile([P, D], BF16, name="x_%d_%d" % (g, s))
-                sample = key_states[s] if g == 0 else query_states[GROUP * (g - 1) + s]
-                nc.sync.dma_start(out=x_tiles[g, s][:], in_=sample)
-
-        def load_weight(w, words, scales):
-            for quadrant in range(4):
-                nc.sync.dma_start(
-                    out=w_scales[32 * quadrant : 32 * quadrant + 4, w, :].bitcast(I32),
-                    in_=scales[0, 4 * quadrant : 4 * quadrant + 4, :].bitcast(I32),
+        def load_x(g, queue=nc.sync, pieces=2):
+            samples = key_states if g == 0 else query_states[GROUP * (g - 1) : GROUP * g]
+            x_tiles[g] = loads.tile([P, GROUP, D], BF16, name="x_%d" % g)
+            size = GROUP // pieces
+            for i in range(pieces):
+                queue.dma_start(
+                    out=x_tiles[g][:, size * i : size * (i + 1), :],
+                    in_=samples[size * i : size * (i + 1)].rearrange("s p d -> p s d"),
                 )
+
+        def load_words(w, words):
             nc.sync.dma_start(
                 out=w_words[:, w, :].bitcast(I32),
                 in_=words[0].rearrange("p n t -> p (n t)").bitcast(I32),
             )
 
+        def load_scales(w, scales):
+            for quadrant in range(4):
+                nc.sync.dma_start(
+                    out=w_scales[32 * quadrant : 32 * quadrant + 4, w, :].bitcast(I32),
+                    in_=scales[0, 4 * quadrant : 4 * quadrant + 4, :].bitcast(I32),
+                )
+
         load_x(0)
-        load_weight(0, Wk_words, Wk_scales)
-        load_x(1)
-        load_weight(1, Wq_words, Wq_scales)
+        nc.scalar.dma_start(out=bias_rows[0][0:PACK, :], in_=bk.rearrange("(j p) -> j p", p=P))
+        load_words(0, Wk_words)
+        load_x(1, nc.scalar, 1)
+        load_scales(0, Wk_scales)
+        nc.sync.dma_start(out=bias_rows[1][0:PACK, :], in_=bq.rearrange("(j p) -> j p", p=P))
+        load_words(1, Wq_words)
+        load_scales(1, Wq_scales)
         for g in range(2, N_GROUPS):
             load_x(g)
-
-        nc.scalar.dma_start(out=bias_rows[0:PACK, :], in_=bk.rearrange("(j p) -> j p", p=P))
-        nc.scalar.dma_start(out=bias_rows[PACK : 2 * PACK, :], in_=bq.rearrange("(j p) -> j p", p=P))
         log_gain = consts.tile([P, 1], BF16)
-        nc.scalar.dma_start(out=log_gain[:], in_=logit_scale.partition_broadcast(P))
+        nc.sync.dma_start(out=log_gain[:], in_=logit_scale.partition_broadcast(P))
 
         bias = consts.tile([P, 2 * PACK], F32)
 
-        def spread_biases():
-            bias_rows_f32 = consts.tile([P, P], F32)
-            nc.vector.tensor_copy(out=bias_rows_f32[:], in_=bias_rows[:])
-            bias_t = psum_q.tile([P, TOKENS], F32, tag="acc")
-            nc.tensor.transpose(bias_t[:, 0:P], bias_rows_f32[:], identity[:])
-            nc.vector.tensor_copy(out=bias[:], in_=bias_t[:, 0 : 2 * PACK])
+        bias_columns = {}
+
+        def transpose_bias(w):
+            rows_f32 = consts.tile([P, P], F32, name="bias_rows_f32_%d" % w)
+            nc.vector.tensor_copy(out=rows_f32[:], in_=bias_rows[w][:])
+            bias_columns[w] = psum_q.tile([P, TOKENS], F32, name="bias_columns", tag="acc")
+            nc.tensor.transpose(bias_columns[w][:, 0:P], rows_f32[:], identity[:])
+
+        def keep_bias(w):
+            nc.vector.tensor_copy(out=bias[:, PACK * w : PACK * (w + 1)], in_=bias_columns[w][:, 0:PACK])
 
         k_codes = consts.tile([P, TOKENS], U32, align_bytes=64)
         k_scales = consts.tile([P, TOKENS], U8, align_bytes=64)
@@ -105,59 +117,63 @@ def tile_attention_pa_t_kernel(
         q_codes = {0: k_codes}
         q_scales = {0: k_scales}
 
-        def transpose_x(g):
-            x_grouped[g] = work.tile([P, TOKENS, PACK], BF16, name="x_grouped", align_bytes=64)
+        def transpose_half(g, half):
+            if half == 0:
+                x_grouped[g] = work.tile([P, TOKENS, PACK], BF16, name="x_grouped", align_bytes=64)
             words_out = x_grouped[g][:].rearrange("p t c -> p (t c)").bitcast(F32).rearrange("p (t u) -> p t u", u=2)
-            for half in range(2):
-                xt = psum_x.tile([P, 2, 2 * P], F32, tag="xt")
-                for s in range(2):
-                    words_in = x_tiles[g, 2 * half + s][:].bitcast(F32)
-                    for u in range(2):
-                        nc.tensor.transpose(xt[:, u, P * s : P * (s + 1)], words_in[:, u : D // 2 : 2], identity[:])
-                nc.scalar.copy(
-                    out=words_out[:, 2 * P * half : 2 * P * (half + 1), :],
-                    in_=xt[:].rearrange("p u t -> p t u"),
-                )
-
-        def quantise_x(g):
-            x_codes[g] = work.tile([P, TOKENS], U32, name="x_codes", align_bytes=64)
-            x_scales[g] = work.tile([P, TOKENS], U8, name="x_scales", align_bytes=64)
-            nc.vector.quantize_mx(
-                out=x_codes[g][:].bitcast(FP8X4),
-                scales=x_scales[g][:],
-                in_=x_grouped[g][:].rearrange("p t c -> p (t c)"),
+            xt = psum_x.tile([P, 2, 2 * P], F32, tag="xt")
+            for s in range(2):
+                words_in = x_tiles[g][:, 2 * half + s, :].bitcast(F32)
+                for u in range(2):
+                    nc.tensor.transpose(xt[:, u, P * s : P * (s + 1)], words_in[:, u : D // 2 : 2], identity[:])
+            nc.scalar.copy(
+                out=words_out[:, HALF * half : HALF * (half + 1), :],
+                in_=xt[:].rearrange("p u t -> p t u"),
             )
 
-        def project(g):
+        def transpose_x(g):
+            for half in range(2):
+                transpose_half(g, half)
+
+        def quantise_x_tokens(g, first, count):
+            if first == 0:
+                x_codes[g] = work.tile([P, TOKENS], U32, name="x_codes", align_bytes=64)
+                x_scales[g] = work.tile([P, TOKENS], U8, name="x_scales", align_bytes=64)
+            nc.vector.quantize_mx(
+                out=x_codes[g][:, first : first + count].bitcast(FP8X4),
+                scales=x_scales[g][:, first : first + count],
+                in_=x_grouped[g][:, first : first + count, :].rearrange("p t c -> p (t c)"),
+            )
+
+        def quantise_x(g):
+            quantise_x_tokens(g, 0, TOKENS)
+
+        def project_tokens(g, j, acc, first, count):
             w = 0 if g == 0 else 1
-            q_planes[g] = work.tile([P, PACK, TOKENS], BF16, name="q_planes")
-            for j in range(PACK):
+            nc.tensor.matmul_mx(
+                out=acc,
+                lhsT=w_words[:, w, P * j : P * (j + 1)].bitcast(FP8X4),
+                lhsT_scale=w_scales[:, w, P * j : P * (j + 1)],
+                rhs=x_codes[g][:, first : first + count].bitcast(FP8X4),
+                rhs_scale=x_scales[g][:, first : first + count],
+                start=True,
+                stop=True,
+            )
+
+        def add_bias(g, j, out, acc):
+            column = (0 if g == 0 else PACK) + j
+            nc.scalar.activation(out=out, in_=acc, func=ACT.Identity, bias=bias[:, column : column + 1], scale=1.0)
+
+        def project(g, features=range(PACK)):
+            if features[0] == 0:
+                q_planes[g] = work.tile([P, PACK, TOKENS], BF16, name="q_planes")
+            for j in features:
                 acc = psum_q.tile([P, TOKENS], F32, tag="acc")
-                nc.tensor.matmul_mx(
-                    out=acc[:],
-                    lhsT=w_words[:, w, P * j : P * (j + 1)].bitcast(FP8X4),
-                    lhsT_scale=w_scales[:, w, P * j : P * (j + 1)],
-                    rhs=x_codes[g][:].bitcast(FP8X4),
-                    rhs_scale=x_scales[g][:],
-                    start=True,
-                    stop=True,
-                )
-                nc.scalar.activation(
-                    out=q_planes[g][:, j, :],
-                    in_=acc[:],
-                    func=ACT.Identity,
-                    bias=bias[:, PACK * w + j : PACK * w + j + 1],
-                    scale=1.0,
-                )
+                project_tokens(g, j, acc[:], 0, TOKENS)
+                add_bias(g, j, q_planes[g][:, j, :], acc[:])
 
         def regroup(g):
             q_grouped[g] = single.tile([P, TOKENS, PACK], BF16, name="q_grouped", align_bytes=64)
-            if g < HEAD_GROUPS:
-                nc.vector.tensor_copy(
-                    out=q_grouped[g][:].rearrange("p (c i) j -> p c j i", i=4),
-                    in_=q_planes[g][:].rearrange("p j (c i) -> p c j i", i=4),
-                )
-                return
             piece = TOKENS // REGROUP_PIECES
             for i in range(REGROUP_PIECES):
                 nc.gpsimd.tensor_scalar(
@@ -168,6 +184,40 @@ def tile_attention_pa_t_kernel(
                     op0=ALU.mult,
                     op1=ALU.add,
                 )
+
+        direct = {}
+
+        def head_group(g):
+            q_grouped[g] = consts.tile([P, TOKENS, PACK], BF16, name="q_grouped_%d" % g, align_bytes=64)
+            q_planes[g] = consts.tile([P, PACK, HALF], BF16, name="q_planes_%d" % g)
+
+        def project_sample(g, s):
+            direct[g, s] = psum_r.tile([P, PACK, P], F32, name="direct", tag="r")
+            for j in range(PACK):
+                project_tokens(g, j, direct[g, s][:, j, :], P * s, P)
+
+        def add_bias_and_group(g, s):
+            w = 0 if g == 0 else 1
+            nc.vector.tensor_tensor(
+                out=q_grouped[g][:, P * s : P * (s + 1), :],
+                in0=direct[g, s][:].rearrange("p j t -> p t j"),
+                in1=bias[:, PACK * w : PACK * (w + 1)].unsqueeze(1).to_broadcast([P, P, PACK]),
+                op=ALU.add,
+            )
+
+        def project_second_half(g):
+            for pair in range(2):
+                acc = psum_q.tile([P, 2, HALF], F32, tag="acc")
+                for i in range(2):
+                    project_tokens(g, 2 * pair + i, acc[:, i, :], HALF, HALF)
+                for i in range(2):
+                    add_bias(g, 2 * pair + i, q_planes[g][:, 2 * pair + i, :], acc[:, i, :])
+
+        def group_second_half(g):
+            nc.vector.tensor_copy(
+                out=q_grouped[g][:, HALF:TOKENS, :].rearrange("p (c i) j -> p c j i", i=4),
+                in_=q_planes[g][:].rearrange("p j (c i) -> p c j i", i=4),
+            )
 
         def quantise_q(g):
             if g > 0:
@@ -218,37 +268,93 @@ def tile_attention_pa_t_kernel(
             )
 
         def when_valid(stage, g):
-            if 0 <= g < N_GROUPS:
+            if g < N_GROUPS:
                 stage(g)
 
-        for g in range(-4, N_GROUPS):
-            if g == -3:
-                spread_biases()
-            if g >= 1:
-                for i in range(4):
-                    max_by_query_token(g, i)
-                    pass_by_key_token(g, i)
-            when_valid(quantise_x, g + 3)
-            when_valid(quantise_q, g + 1)
-            when_valid(transpose_x, g + 4)
-            when_valid(regroup, g + 2)
+        def halves_quantised(g):
+            for half in range(2):
+                quantise_x_tokens(g, HALF * half, HALF)
+
+        head_group(0)
+        head_group(1)
+        transpose_x(0)
+        transpose_bias(0)
+        quantise_x_tokens(0, 0, HALF)
+        keep_bias(0)
+        quantise_x_tokens(0, HALF, HALF)
+        transpose_half(1, 0)
+        project_sample(0, 0)
+        transpose_bias(1)
+        transpose_half(1, 1)
+        project_sample(0, 1)
+        add_bias_and_group(0, 0)
+        keep_bias(1)
+        project_second_half(0)
+        quantise_x_tokens(1, 0, HALF)
+        add_bias_and_group(0, 1)
+        quantise_x_tokens(1, HALF, HALF)
+        project_sample(1, 0)
+        project_sample(1, 1)
+        project_second_half(1)
+        transpose_x(2)
+        add_bias_and_group(1, 0)
+        add_bias_and_group(1, 1)
+        group_second_half(0)
+        quantise_q(0)
+        group_second_half(1)
+        quantise_q(1)
+        quantise_x(2)
+        transpose_x(3)
+        for i in range(4):
+            pass_by_query_token(1, i)
+        project(2, (0, 1))
+
+        for i in range(4):
+            max_by_query_token(1, i)
+            pass_by_key_token(1, i)
+            if i < 2:
+                project(2, (2 + i,))
+        regroup(2)
+        max_by_key_token(1, 0)
+        quantise_x(3)
+        transpose_x(4)
+        project(3, (0, 1))
+        max_by_key_token(1, 1)
+        max_by_key_token(1, 2)
+        project(3, (2, 3))
+
+        for g in range(2, N_GROUPS):
+            when_valid(quantise_x, g + 2)
+            quantise_q(g)
+            when_valid(transpose_x, g + 3)
+            when_valid(regroup, g + 1)
             for i in range(4):
-                if g >= 1:
-                    max_by_key_token(g, i)
-                if 1 <= g + 1 < N_GROUPS:
-                    pass_by_query_token(g + 1, i)
-            when_valid(project, g + 3)
+                if g > 2 or i == 3:
+                    max_by_key_token(g - 1, i)
+                pass_by_query_token(g, i)
+            for i in range(4):
+                max_by_query_token(g, i)
+                pass_by_key_token(g, i)
+                if g + 2 < N_GROUPS:
+                    project(g + 2, (i,))
+        for i in range(4):
+            max_by_key_token(N_GROUPS - 1, i)
 
         gain = consts.tile([P, 1], F32)
         nc.scalar.activation(out=gain[:], in_=log_gain[:], func=ACT.Exp)
         means = psum_q.tile([P, TOKENS], F32, tag="acc")
-        means_flat = means[:, 0 : N_QUERY * N_KEY]
-        nc.tensor.matmul(
-            out=means_flat, lhsT=mean_weights[:], rhs=row_max[:].rearrange("p a b -> p (a b)"), start=True, stop=False
-        )
-        nc.tensor.matmul(
-            out=means_flat, lhsT=mean_weights[:], rhs=col_max[:].rearrange("p a b -> p (a b)"), start=False, stop=True
-        )
+        last = GROUP * (N_STEPS - 1)
+        for first, end in ((0, last), (last, N_QUERY)):
+            for maxima in (row_max, col_max):
+                nc.tensor.matmul(
+                    out=means[:, N_KEY * first : N_KEY * end],
+                    lhsT=mean_weights[:],
+                    rhs=maxima[:, first:end, :].rearrange("p a b -> p (a b)"),
+                    start=maxima is row_max,
+                    stop=maxima is col_max,
+                )
         result = consts.tile([P, N_QUERY * N_KEY], F32)
-        nc.scalar.activation(out=result[:], in_=means_flat, func=ACT.Copy, scale=gain[:, 0:1])
+        nc.scalar.activation(
+            out=result[:], in_=means[:, 0 : N_QUERY * N_KEY], func=ACT.Copy, scale=gain[:, 0:1]
+        )
         nc.sync.dma_start(out=out.rearrange("a b -> (a b)").unsqueeze(0), in_=result[0:1, :])

@@ -22,7 +22,6 @@ GROUP = 4
 TOKENS = GROUP * P
 HALF = TOKENS // 2
 N_STEPS = N_QUERY // GROUP
-REGROUP_PIECES = 2
 N_GROUPS = N_STEPS + 1
 
 FLOPS = 2 * (N_QUERY + N_KEY) * P * D * D + 2 * N_QUERY * P * N_KEY * P * D
@@ -174,16 +173,23 @@ def tile_attention_pa_t_kernel(
 
         def regroup(g):
             q_grouped[g] = single.tile([P, TOKENS, PACK], BF16, name="q_grouped", align_bytes=64)
-            piece = TOKENS // REGROUP_PIECES
-            for i in range(REGROUP_PIECES):
-                nc.gpsimd.tensor_scalar(
-                    out=q_grouped[g][:, piece * i : piece * (i + 1), :],
-                    in0=q_planes[g][:, :, piece * i : piece * (i + 1)].rearrange("p j t -> p t j"),
-                    scalar1=1.0,
-                    scalar2=0.0,
-                    op0=ALU.mult,
-                    op1=ALU.add,
-                )
+            for half in range(2):
+                grouped = q_grouped[g][:, HALF * half : HALF * (half + 1), :]
+                planes = q_planes[g][:, :, HALF * half : HALF * (half + 1)]
+                if half == 0 and g > 2:
+                    nc.scalar.copy(
+                        out=grouped.rearrange("p (c i) j -> p c j i", i=4),
+                        in_=planes.rearrange("p j (c i) -> p c j i", i=4),
+                    )
+                else:
+                    nc.gpsimd.tensor_scalar(
+                        out=grouped,
+                        in0=planes.rearrange("p j t -> p t j"),
+                        scalar1=1.0,
+                        scalar2=0.0,
+                        op0=ALU.mult,
+                        op1=ALU.add,
+                    )
 
         direct = {}
 
@@ -326,8 +332,8 @@ def tile_attention_pa_t_kernel(
         for g in range(2, N_GROUPS):
             when_valid(quantise_x, g + 2)
             quantise_q(g)
-            when_valid(transpose_x, g + 3)
             when_valid(regroup, g + 1)
+            when_valid(transpose_x, g + 3)
             for i in range(4):
                 if g > 2 or i == 3:
                     max_by_key_token(g - 1, i)

@@ -21,6 +21,10 @@ N_KEY = 4
 GROUP = 4
 TOKENS = GROUP * P
 HALF = TOKENS // 2
+REGROUP_SHARES = (("scalar", 128), ("gpsimd", 320), ("gpsimd", 512))
+HEAD_REGROUP_SHARES = (("gpsimd", 256), ("gpsimd", 512))
+PAIRED_SAMPLES = (1,)
+FIRST_PAIRED = 3
 N_STEPS = N_QUERY // GROUP
 N_GROUPS = N_STEPS + 1
 
@@ -173,10 +177,11 @@ def tile_attention_pa_t_kernel(
 
         def regroup(g):
             q_grouped[g] = single.tile([P, TOKENS, PACK], BF16, name="q_grouped", align_bytes=64)
-            for half in range(2):
-                grouped = q_grouped[g][:, HALF * half : HALF * (half + 1), :]
-                planes = q_planes[g][:, :, HALF * half : HALF * (half + 1)]
-                if half == 0 and g > 2:
+            first = 0
+            for engine, end in REGROUP_SHARES if g > 2 else HEAD_REGROUP_SHARES:
+                grouped = q_grouped[g][:, first:end, :]
+                planes = q_planes[g][:, :, first:end]
+                if engine == "scalar":
                     nc.scalar.copy(
                         out=grouped.rearrange("p (c i) j -> p c j i", i=4),
                         in_=planes.rearrange("p j (c i) -> p c j i", i=4),
@@ -190,6 +195,7 @@ def tile_attention_pa_t_kernel(
                         op0=ALU.mult,
                         op1=ALU.add,
                     )
+                first = end
 
         direct = {}
 
@@ -253,6 +259,69 @@ def tile_attention_pa_t_kernel(
         def max_by_query_token(g, s):
             nc.vector.tensor_reduce(
                 out=row_max[:, GROUP * (g - 1) + s, :], in_=banks["query", g, s][:], axis=AXIS_X, op=ALU.max
+            )
+
+        pair_codes = consts.tile([P, 3, HALF], U32, align_bytes=64)
+        pair_scales = consts.tile([P, 3, HALF], U8, align_bytes=64)
+        negated = consts.tile([P, HALF, PACK], BF16, align_bytes=64)
+
+        def pair_keys():
+            for half in range(2):
+                for pairs_of, keys_of in ((pair_codes, k_codes), (pair_scales, k_scales)):
+                    as_moved = I32 if pairs_of is pair_codes else U8
+                    nc.vector.tensor_copy(
+                        out=pairs_of[:, 1 - half, :].bitcast(as_moved).rearrange("p (b m) -> p b m", b=N_KEY),
+                        in_=keys_of[:].bitcast(as_moved).rearrange("p (b h m) -> p h b m", b=N_KEY, h=2)[:, half],
+                    )
+            nc.vector.tensor_scalar(
+                out=negated[:].rearrange("p (b m) j -> p b (m j)", b=N_KEY),
+                in0=q_grouped[0][:].rearrange("p (b h m) j -> p h b (m j)", b=N_KEY, h=2)[:, 1],
+                scalar1=-1.0,
+                scalar2=None,
+                op0=ALU.mult,
+            )
+
+        def quantise_pairs():
+            nc.vector.quantize_mx(
+                out=pair_codes[:, 2, :].bitcast(FP8X4),
+                scales=pair_scales[:, 2, :],
+                in_=negated[:].rearrange("p t c -> p (t c)"),
+            )
+
+        def paired(g, s):
+            return FIRST_PAIRED <= g < N_GROUPS - 1 and s in PAIRED_SAMPLES
+
+        pairs = {}
+        pair_max = {}
+
+        def pass_by_pairs(g, s):
+            r = psum_r.tile([P, 2, HALF], F32, tag="r")
+            for piece, half, start, stop in ((0, 0, True, True), (1, 1, True, False), (2, 1, False, True)):
+                nc.tensor.matmul_mx(
+                    out=r[:, half, :],
+                    lhsT=q_codes[g][:, P * s : P * (s + 1)].bitcast(FP8X4),
+                    lhsT_scale=q_scales[g][:, P * s : P * (s + 1)],
+                    rhs=pair_codes[:, piece, :].bitcast(FP8X4),
+                    rhs_scale=pair_scales[:, piece, :],
+                    start=start,
+                    stop=stop,
+                )
+            pairs[g, s] = work.tile([P, 2, HALF], F32, name="pairs_%d" % s)
+            nc.scalar.copy(out=pairs[g, s][:, 0, :], in_=r[:, 0, :])
+            nc.scalar.activation(out=pairs[g, s][:, 1, :], in_=r[:, 1, :], func=ACT.Relu)
+
+        def max_of_pairs(g, s):
+            pair_max[g, s] = work.tile([P, N_KEY, P // 2], F32, name="pair_max_%d" % s)
+            nc.gpsimd.tensor_tensor(
+                out=pair_max[g, s][:].rearrange("p b m -> p (b m)"),
+                in0=pairs[g, s][:, 0, :],
+                in1=pairs[g, s][:, 1, :],
+                op=ALU.add,
+            )
+
+        def max_by_query_token_of_pairs(g, s):
+            nc.vector.tensor_reduce(
+                out=row_max[:, GROUP * (g - 1) + s, :], in_=pair_max[g, s][:], axis=AXIS_X, op=ALU.max
             )
 
         def pass_by_key_token(g, b):
@@ -328,18 +397,35 @@ def tile_attention_pa_t_kernel(
         max_by_key_token(1, 1)
         max_by_key_token(1, 2)
         project(3, (2, 3))
+        pair_keys()
+
+        def last_paired(g):
+            for s in range(GROUP):
+                if paired(g, s):
+                    max_by_query_token_of_pairs(g, s)
 
         for g in range(2, N_GROUPS):
             when_valid(quantise_x, g + 2)
             quantise_q(g)
+            if g == FIRST_PAIRED - 1:
+                quantise_pairs()
             when_valid(regroup, g + 1)
             when_valid(transpose_x, g + 3)
             for i in range(4):
                 if g > 2 or i == 3:
                     max_by_key_token(g - 1, i)
-                pass_by_query_token(g, i)
+                if paired(g, i):
+                    pass_by_pairs(g, i)
+                else:
+                    pass_by_query_token(g, i)
+                if i == 2:
+                    last_paired(g - 1)
             for i in range(4):
-                max_by_query_token(g, i)
+                if paired(g, i):
+                    max_of_pairs(g, i)
+            for i in range(4):
+                if not paired(g, i):
+                    max_by_query_token(g, i)
                 pass_by_key_token(g, i)
                 if g + 2 < N_GROUPS:
                     project(g + 2, (i,))

@@ -22,7 +22,7 @@ GROUP = 4
 TOKENS = GROUP * P
 HALF = TOKENS // 2
 REGROUP_SHARES = (("scalar", 128), ("gpsimd", 320), ("gpsimd", 512))
-HEAD_REGROUP_SHARES = (("gpsimd", 256), ("gpsimd", 512))
+HEAD_REGROUP_SHARES = (("gpsimd", 192), ("gpsimd", 384), ("vector", 512))
 PAIRED_SAMPLES = (1,)
 FIRST_PAIRED = 3
 N_STEPS = N_QUERY // GROUP
@@ -181,11 +181,12 @@ def tile_attention_pa_t_kernel(
             for engine, end in REGROUP_SHARES if g > 2 else HEAD_REGROUP_SHARES:
                 grouped = q_grouped[g][:, first:end, :]
                 planes = q_planes[g][:, :, first:end]
+                out_by_four = grouped.rearrange("p (c i) j -> p c j i", i=4)
+                in_by_four = planes.rearrange("p j (c i) -> p c j i", i=4)
                 if engine == "scalar":
-                    nc.scalar.copy(
-                        out=grouped.rearrange("p (c i) j -> p c j i", i=4),
-                        in_=planes.rearrange("p j (c i) -> p c j i", i=4),
-                    )
+                    nc.scalar.copy(out=out_by_four, in_=in_by_four)
+                elif engine == "vector":
+                    nc.vector.tensor_copy(out=out_by_four, in_=in_by_four)
                 else:
                     nc.gpsimd.tensor_scalar(
                         out=grouped,
@@ -379,6 +380,7 @@ def tile_attention_pa_t_kernel(
         group_second_half(1)
         quantise_q(1)
         quantise_x(2)
+        pair_keys()
         transpose_x(3)
         for i in range(4):
             pass_by_query_token(1, i)
@@ -389,7 +391,6 @@ def tile_attention_pa_t_kernel(
             pass_by_key_token(1, i)
             if i < 2:
                 project(2, (2 + i,))
-        regroup(2)
         max_by_key_token(1, 0)
         quantise_x(3)
         transpose_x(4)
@@ -397,7 +398,7 @@ def tile_attention_pa_t_kernel(
         max_by_key_token(1, 1)
         max_by_key_token(1, 2)
         project(3, (2, 3))
-        pair_keys()
+        regroup(2)
 
         def last_paired(g):
             for s in range(GROUP):
@@ -426,9 +427,9 @@ def tile_attention_pa_t_kernel(
             for i in range(4):
                 if not paired(g, i):
                     max_by_query_token(g, i)
-                pass_by_key_token(g, i)
                 if g + 2 < N_GROUPS:
                     project(g + 2, (i,))
+                pass_by_key_token(g, i)
         for i in range(4):
             max_by_key_token(N_GROUPS - 1, i)
 

@@ -22,8 +22,10 @@ GROUP = 4
 TOKENS = GROUP * P
 HALF = TOKENS // 2
 REGROUP_SHARES = (("scalar", 128), ("gpsimd", 320), ("gpsimd", 512))
+LAST_REGROUP_SHARES = (("scalar", 256), ("gpsimd", 512))
 HEAD_REGROUP_SHARES = (("gpsimd", 192), ("gpsimd", 384), ("vector", 512))
 PAIRED_SAMPLES = (1,)
+PAIRED_SAMPLES_AT_THE_END = {0: (0, 1, 2, 3), 1: (1, 2, 3)}
 FIRST_PAIRED = 3
 N_STEPS = N_QUERY // GROUP
 N_GROUPS = N_STEPS + 1
@@ -178,7 +180,8 @@ def tile_attention_pa_t_kernel(
         def regroup(g):
             q_grouped[g] = single.tile([P, TOKENS, PACK], BF16, name="q_grouped", align_bytes=64)
             first = 0
-            for engine, end in REGROUP_SHARES if g > 2 else HEAD_REGROUP_SHARES:
+            shares = REGROUP_SHARES if 2 < g < N_GROUPS - 2 else HEAD_REGROUP_SHARES if g == 2 else LAST_REGROUP_SHARES
+            for engine, end in shares:
                 grouped = q_grouped[g][:, first:end, :]
                 planes = q_planes[g][:, :, first:end]
                 out_by_four = grouped.rearrange("p (c i) j -> p c j i", i=4)
@@ -290,7 +293,7 @@ def tile_attention_pa_t_kernel(
             )
 
         def paired(g, s):
-            return FIRST_PAIRED <= g < N_GROUPS - 1 and s in PAIRED_SAMPLES
+            return g >= FIRST_PAIRED and s in PAIRED_SAMPLES_AT_THE_END.get(N_GROUPS - 1 - g, PAIRED_SAMPLES)
 
         pairs = {}
         pair_max = {}
@@ -419,8 +422,7 @@ def tile_attention_pa_t_kernel(
                     pass_by_pairs(g, i)
                 else:
                     pass_by_query_token(g, i)
-                if i == 2:
-                    last_paired(g - 1)
+            last_paired(g - 1)
             for i in range(4):
                 if paired(g, i):
                     max_of_pairs(g, i)
@@ -432,19 +434,20 @@ def tile_attention_pa_t_kernel(
                 pass_by_key_token(g, i)
         for i in range(4):
             max_by_key_token(N_GROUPS - 1, i)
+        last_paired(N_GROUPS - 1)
 
         gain = consts.tile([P, 1], F32)
         nc.scalar.activation(out=gain[:], in_=log_gain[:], func=ACT.Exp)
         means = psum_q.tile([P, TOKENS], F32, tag="acc")
         last = GROUP * (N_STEPS - 1)
         for first, end in ((0, last), (last, N_QUERY)):
-            for maxima in (row_max, col_max):
+            for maxima in (col_max, row_max):
                 nc.tensor.matmul(
                     out=means[:, N_KEY * first : N_KEY * end],
                     lhsT=mean_weights[:],
                     rhs=maxima[:, first:end, :].rearrange("p a b -> p (a b)"),
-                    start=maxima is row_max,
-                    stop=maxima is col_max,
+                    start=maxima is col_max,
+                    stop=maxima is row_max,
                 )
         result = consts.tile([P, N_QUERY * N_KEY], F32)
         nc.scalar.activation(

@@ -438,19 +438,23 @@ def tile_attention_pa_t_kernel(
 
         gain = consts.tile([P, 1], F32)
         nc.scalar.activation(out=gain[:], in_=log_gain[:], func=ACT.Exp)
-        means = psum_q.tile([P, TOKENS], F32, tag="acc")
+        result = consts.tile([P, N_QUERY, N_KEY], F32)
         last = GROUP * (N_STEPS - 1)
         for first, end in ((0, last), (last, N_QUERY)):
+            means = psum_q.tile([P, TOKENS], F32, tag="acc")
+            means_of_part = means[:, 0 : N_KEY * (end - first)]
             for maxima in (col_max, row_max):
                 nc.tensor.matmul(
-                    out=means[:, N_KEY * first : N_KEY * end],
+                    out=means_of_part,
                     lhsT=mean_weights[:],
                     rhs=maxima[:, first:end, :].rearrange("p a b -> p (a b)"),
                     start=maxima is col_max,
                     stop=maxima is row_max,
                 )
-        result = consts.tile([P, N_QUERY * N_KEY], F32)
-        nc.scalar.activation(
-            out=result[:], in_=means[:, 0 : N_QUERY * N_KEY], func=ACT.Copy, scale=gain[:, 0:1]
-        )
-        nc.sync.dma_start(out=out.rearrange("a b -> (a b)").unsqueeze(0), in_=result[0:1, :])
+            nc.scalar.activation(
+                out=result[:, first:end, :].rearrange("p a b -> p (a b)"),
+                in_=means_of_part,
+                func=ACT.Copy,
+                scale=gain[:, 0:1],
+            )
+        nc.sync.dma_start(out=out.rearrange("a b -> (a b)").unsqueeze(0), in_=result[0:1].rearrange("p a b -> p (a b)"))

from contextlib import ExitStack

import concourse.mybir as mybir
from concourse.masks import make_identity

F32 = mybir.dt.float32
BF16 = mybir.dt.bfloat16
I32 = mybir.dt.int32
U32 = mybir.dt.uint32
U8 = mybir.dt.uint8
FP8X4 = mybir.dt.float8_e4m3fn_x4
ACT = mybir.ActivationFunctionType
ALU = mybir.AluOpType
AXIS_X = mybir.AxisListType.X

P = 128
PACK = 4
D = P * PACK
N_QUERY = 64
N_KEY = 4
GROUP = 4
TOKENS = GROUP * P
HALF = TOKENS // 2
REGROUP_SHARES = (("scalar", 128), ("gpsimd", 320), ("gpsimd", 512))
LAST_REGROUP_SHARES = (("scalar", 256), ("gpsimd", 512))
HEAD_REGROUP_SHARES = (("gpsimd", 192), ("gpsimd", 384), ("vector", 512))
PAIRED_SAMPLES = (1,)
PAIRED_SAMPLES_AT_THE_END = {0: (0, 1, 2, 3), 1: (1, 2, 3)}
FIRST_PAIRED = 3
N_STEPS = N_QUERY // GROUP
N_GROUPS = N_STEPS + 1

FLOPS = 2 * (N_QUERY + N_KEY) * P * D * D + 2 * N_QUERY * P * N_KEY * P * D


def tile_attention_pa_t_kernel(
    tc, query_states, key_states, Wq_words, Wq_scales, bq, Wk_words, Wk_scales, bk, logit_scale, out
):
    nc = tc.nc
    with ExitStack() as stack:
        consts = stack.enter_context(tc.tile_pool(name="consts", bufs=1))
        loads = stack.enter_context(tc.tile_pool(name="loads", bufs=1))
        work = stack.enter_context(tc.tile_pool(name="work", bufs=2))
        single = stack.enter_context(tc.tile_pool(name="single", bufs=1))
        psum_x = stack.enter_context(tc.psum_pool(name="psum_x", bufs=2))
        psum_q = stack.enter_context(tc.psum_pool(name="psum_q", bufs=2))
        psum_r = stack.enter_context(tc.psum_pool(name="psum_r", bufs=4))
        stack.enter_context(tc.manual_schedule())

        w_scales = consts.tile([P, 2, D], U8, align_bytes=64)
        nc.vector.memset(w_scales[:].rearrange("p w n -> p (w n)").bitcast(I32), 0)
        bias_rows = [consts.tile([P, P], BF16, name="bias_rows_%d" % w) for w in range(2)]
        for w in range(2):
            nc.vector.memset(bias_rows[w][:], 0.0)
        mean_weights = consts.tile([P, P], F32)
        nc.vector.memset(mean_weights[:], 1.0 / (2 * P))
        identity = consts.tile([P, P], F32)
        make_identity(nc, identity[:])

        x_tiles = {}
        w_words = consts.tile([P, 2, D], U32, align_bytes=64)

        def load_x(g, queue=nc.sync, pieces=2):
            samples = key_states if g == 0 else query_states[GROUP * (g - 1) : GROUP * g]
            x_tiles[g] = loads.tile([P, GROUP, D], BF16, name="x_%d" % g)
            size = GROUP // pieces
            for i in range(pieces):
                queue.dma_start(
                    out=x_tiles[g][:, size * i : size * (i + 1), :],
                    in_=samples[size * i : size * (i + 1)].rearrange("s p d -> p s d"),
                )

        def load_words(w, words):
            nc.sync.dma_start(
                out=w_words[:, w, :].bitcast(I32),
                in_=words[0].rearrange("p n t -> p (n t)").bitcast(I32),
            )

        def load_scales(w, scales):
            for quadrant in range(4):
                nc.sync.dma_start(
                    out=w_scales[32 * quadrant : 32 * quadrant + 4, w, :].bitcast(I32),
                    in_=scales[0, 4 * quadrant : 4 * quadrant + 4, :].bitcast(I32),
                )

        load_x(0)
        nc.scalar.dma_start(out=bias_rows[0][0:PACK, :], in_=bk.rearrange("(j p) -> j p", p=P))
        load_words(0, Wk_words)
        load_x(1, nc.scalar, 1)
        load_scales(0, Wk_scales)
        nc.sync.dma_start(out=bias_rows[1][0:PACK, :], in_=bq.rearrange("(j p) -> j p", p=P))
        load_words(1, Wq_words)
        load_scales(1, Wq_scales)
        for g in range(2, N_GROUPS):
            load_x(g)
        log_gain = consts.tile([P, 1], BF16)
        nc.sync.dma_start(out=log_gain[:], in_=logit_scale.partition_broadcast(P))

        bias = consts.tile([P, 2 * PACK], F32)

        bias_columns = {}

        def transpose_bias(w):
            rows_f32 = consts.tile([P, P], F32, name="bias_rows_f32_%d" % w)
            nc.vector.tensor_copy(out=rows_f32[:], in_=bias_rows[w][:])
            bias_columns[w] = psum_q.tile([P, TOKENS], F32, name="bias_columns", tag="acc")
            nc.tensor.transpose(bias_columns[w][:, 0:P], rows_f32[:], identity[:])

        def keep_bias(w):
            nc.vector.tensor_copy(out=bias[:, PACK * w : PACK * (w + 1)], in_=bias_columns[w][:, 0:PACK])

        k_codes = consts.tile([P, TOKENS], U32, align_bytes=64)
        k_scales = consts.tile([P, TOKENS], U8, align_bytes=64)
        row_max = consts.tile([P, N_QUERY, N_KEY], F32)
        col_max = consts.tile([P, N_QUERY, N_KEY], F32)

        x_grouped = {}
        x_codes = {}
        x_scales = {}
        q_planes = {}
        q_grouped = {}
        q_codes = {0: k_codes}
        q_scales = {0: k_scales}

        def transpose_half(g, half):
            if half == 0:
                x_grouped[g] = work.tile([P, TOKENS, PACK], BF16, name="x_grouped", align_bytes=64)
            words_out = x_grouped[g][:].rearrange("p t c -> p (t c)").bitcast(F32).rearrange("p (t u) -> p t u", u=2)
            xt = psum_x.tile([P, 2, 2 * P], F32, tag="xt")
            for s in range(2):
                words_in = x_tiles[g][:, 2 * half + s, :].bitcast(F32)
                for u in range(2):
                    nc.tensor.transpose(xt[:, u, P * s : P * (s + 1)], words_in[:, u : D // 2 : 2], identity[:])
            nc.scalar.copy(
                out=words_out[:, HALF * half : HALF * (half + 1), :],
                in_=xt[:].rearrange("p u t -> p t u"),
            )

        def transpose_x(g):
            for half in range(2):
                transpose_half(g, half)

        def quantise_x_tokens(g, first, count):
            if first == 0:
                x_codes[g] = work.tile([P, TOKENS], U32, name="x_codes", align_bytes=64)
                x_scales[g] = work.tile([P, TOKENS], U8, name="x_scales", align_bytes=64)
            nc.vector.quantize_mx(
                out=x_codes[g][:, first : first + count].bitcast(FP8X4),
                scales=x_scales[g][:, first : first + count],
                in_=x_grouped[g][:, first : first + count, :].rearrange("p t c -> p (t c)"),
            )

        def quantise_x(g):
            quantise_x_tokens(g, 0, TOKENS)

        def project_tokens(g, j, acc, first, count):
            w = 0 if g == 0 else 1
            nc.tensor.matmul_mx(
                out=acc,
                lhsT=w_words[:, w, P * j : P * (j + 1)].bitcast(FP8X4),
                lhsT_scale=w_scales[:, w, P * j : P * (j + 1)],
                rhs=x_codes[g][:, first : first + count].bitcast(FP8X4),
                rhs_scale=x_scales[g][:, first : first + count],
                start=True,
                stop=True,
            )

        def add_bias(g, j, out, acc):
            column = (0 if g == 0 else PACK) + j
            nc.scalar.activation(out=out, in_=acc, func=ACT.Identity, bias=bias[:, column : column + 1], scale=1.0)

        def project(g, features=range(PACK)):
            if features[0] == 0:
                q_planes[g] = work.tile([P, PACK, TOKENS], BF16, name="q_planes")
            for j in features:
                acc = psum_q.tile([P, TOKENS], F32, tag="acc")
                project_tokens(g, j, acc[:], 0, TOKENS)
                add_bias(g, j, q_planes[g][:, j, :], acc[:])

        def regroup(g):
            q_grouped[g] = single.tile([P, TOKENS, PACK], BF16, name="q_grouped", align_bytes=64)
            first = 0
            shares = REGROUP_SHARES if 2 < g < N_GROUPS - 2 else HEAD_REGROUP_SHARES if g == 2 else LAST_REGROUP_SHARES
            for engine, end in shares:
                grouped = q_grouped[g][:, first:end, :]
                planes = q_planes[g][:, :, first:end]
                out_by_four = grouped.rearrange("p (c i) j -> p c j i", i=4)
                in_by_four = planes.rearrange("p j (c i) -> p c j i", i=4)
                if engine == "scalar":
                    nc.scalar.copy(out=out_by_four, in_=in_by_four)
                elif engine == "vector":
                    nc.vector.tensor_copy(out=out_by_four, in_=in_by_four)
                else:
                    nc.gpsimd.tensor_scalar(
                        out=grouped,
                        in0=planes.rearrange("p j t -> p t j"),
                        scalar1=1.0,
                        scalar2=0.0,
                        op0=ALU.mult,
                        op1=ALU.add,
                    )
                first = end

        direct = {}

        def head_group(g):
            q_grouped[g] = consts.tile([P, TOKENS, PACK], BF16, name="q_grouped_%d" % g, align_bytes=64)
            q_planes[g] = consts.tile([P, PACK, HALF], BF16, name="q_planes_%d" % g)

        def project_sample(g, s):
            direct[g, s] = psum_r.tile([P, PACK, P], F32, name="direct", tag="r")
            for j in range(PACK):
                project_tokens(g, j, direct[g, s][:, j, :], P * s, P)

        def add_bias_and_group(g, s):
            w = 0 if g == 0 else 1
            nc.vector.tensor_tensor(
                out=q_grouped[g][:, P * s : P * (s + 1), :],
                in0=direct[g, s][:].rearrange("p j t -> p t j"),
                in1=bias[:, PACK * w : PACK * (w + 1)].unsqueeze(1).to_broadcast([P, P, PACK]),
                op=ALU.add,
            )

        def project_second_half(g):
            for pair in range(2):
                acc = psum_q.tile([P, 2, HALF], F32, tag="acc")
                for i in range(2):
                    project_tokens(g, 2 * pair + i, acc[:, i, :], HALF, HALF)
                for i in range(2):
                    add_bias(g, 2 * pair + i, q_planes[g][:, 2 * pair + i, :], acc[:, i, :])

        def group_second_half(g):
            nc.vector.tensor_copy(
                out=q_grouped[g][:, HALF:TOKENS, :].rearrange("p (c i) j -> p c j i", i=4),
                in_=q_planes[g][:].rearrange("p j (c i) -> p c j i", i=4),
            )

        def quantise_q(g):
            if g > 0:
                q_codes[g] = work.tile([P, TOKENS], U32, name="q_codes", align_bytes=64)
                q_scales[g] = work.tile([P, TOKENS], U8, name="q_scales", align_bytes=64)
            nc.vector.quantize_mx(
                out=q_codes[g][:].bitcast(FP8X4),
                scales=q_scales[g][:],
                in_=q_grouped[g][:].rearrange("p t c -> p (t c)"),
            )

        banks = {}

        def pass_by_query_token(g, s):
            r = psum_r.tile([P, N_KEY, P], F32, tag="r")
            nc.tensor.matmul_mx(
                out=r[:].rearrange("l b m -> l (b m)"),
                lhsT=q_codes[g][:, P * s : P * (s + 1)].bitcast(FP8X4),
                lhsT_scale=q_scales[g][:, P * s : P * (s + 1)],
                rhs=k_codes[:].bitcast(FP8X4),
                rhs_scale=k_scales[:],
                start=True,
                stop=True,
            )
            banks["query", g, s] = r

        def max_by_query_token(g, s):
            nc.vector.tensor_reduce(
                out=row_max[:, GROUP * (g - 1) + s, :], in_=banks["query", g, s][:], axis=AXIS_X, op=ALU.max
            )

        pair_codes = consts.tile([P, 3, HALF], U32, align_bytes=64)
        pair_scales = consts.tile([P, 3, HALF], U8, align_bytes=64)
        negated = consts.tile([P, HALF, PACK], BF16, align_bytes=64)

        def pair_keys():
            for half in range(2):
                for pairs_of, keys_of in ((pair_codes, k_codes), (pair_scales, k_scales)):
                    as_moved = I32 if pairs_of is pair_codes else U8
                    nc.vector.tensor_copy(
                        out=pairs_of[:, 1 - half, :].bitcast(as_moved).rearrange("p (b m) -> p b m", b=N_KEY),
                        in_=keys_of[:].bitcast(as_moved).rearrange("p (b h m) -> p h b m", b=N_KEY, h=2)[:, half],
                    )
            nc.vector.tensor_scalar(
                out=negated[:].rearrange("p (b m) j -> p b (m j)", b=N_KEY),
                in0=q_grouped[0][:].rearrange("p (b h m) j -> p h b (m j)", b=N_KEY, h=2)[:, 1],
                scalar1=-1.0,
                scalar2=None,
                op0=ALU.mult,
            )

        def quantise_pairs():
            nc.vector.quantize_mx(
                out=pair_codes[:, 2, :].bitcast(FP8X4),
                scales=pair_scales[:, 2, :],
                in_=negated[:].rearrange("p t c -> p (t c)"),
            )

        def paired(g, s):
            return g >= FIRST_PAIRED and s in PAIRED_SAMPLES_AT_THE_END.get(N_GROUPS - 1 - g, PAIRED_SAMPLES)

        pairs = {}
        pair_max = {}

        def pass_by_pairs(g, s):
            r = psum_r.tile([P, 2, HALF], F32, tag="r")
            for piece, half, start, stop in ((0, 0, True, True), (1, 1, True, False), (2, 1, False, True)):
                nc.tensor.matmul_mx(
                    out=r[:, half, :],
                    lhsT=q_codes[g][:, P * s : P * (s + 1)].bitcast(FP8X4),
                    lhsT_scale=q_scales[g][:, P * s : P * (s + 1)],
                    rhs=pair_codes[:, piece, :].bitcast(FP8X4),
                    rhs_scale=pair_scales[:, piece, :],
                    start=start,
                    stop=stop,
                )
            pairs[g, s] = work.tile([P, 2, HALF], F32, name="pairs_%d" % s)
            nc.scalar.copy(out=pairs[g, s][:, 0, :], in_=r[:, 0, :])
            nc.scalar.activation(out=pairs[g, s][:, 1, :], in_=r[:, 1, :], func=ACT.Relu)

        def max_of_pairs(g, s):
            pair_max[g, s] = work.tile([P, N_KEY, P // 2], F32, name="pair_max_%d" % s)
            nc.gpsimd.tensor_tensor(
                out=pair_max[g, s][:].rearrange("p b m -> p (b m)"),
                in0=pairs[g, s][:, 0, :],
                in1=pairs[g, s][:, 1, :],
                op=ALU.add,
            )

        def max_by_query_token_of_pairs(g, s):
            nc.vector.tensor_reduce(
                out=row_max[:, GROUP * (g - 1) + s, :], in_=pair_max[g, s][:], axis=AXIS_X, op=ALU.max
            )

        def pass_by_key_token(g, b):
            r = psum_r.tile([P, GROUP, P], F32, tag="r")
            nc.tensor.matmul_mx(
                out=r[:].rearrange("m a l -> m (a l)"),
                lhsT=k_codes[:, P * b : P * (b + 1)].bitcast(FP8X4),
                lhsT_scale=k_scales[:, P * b : P * (b + 1)],
                rhs=q_codes[g][:].bitcast(FP8X4),
                rhs_scale=q_scales[g][:],
                start=True,
                stop=True,
            )
            banks["key", g, b] = r

        def max_by_key_token(g, b):
            nc.vector.tensor_reduce(
                out=col_max[:, GROUP * (g - 1) : GROUP * g, b], in_=banks["key", g, b][:], axis=AXIS_X, op=ALU.max
            )

        def when_valid(stage, g):
            if g < N_GROUPS:
                stage(g)

        def halves_quantised(g):
            for half in range(2):
                quantise_x_tokens(g, HALF * half, HALF)

        head_group(0)
        head_group(1)
        transpose_x(0)
        transpose_bias(0)
        quantise_x_tokens(0, 0, HALF)
        keep_bias(0)
        quantise_x_tokens(0, HALF, HALF)
        transpose_half(1, 0)
        project_sample(0, 0)
        transpose_bias(1)
        transpose_half(1, 1)
        project_sample(0, 1)
        add_bias_and_group(0, 0)
        keep_bias(1)
        project_second_half(0)
        quantise_x_tokens(1, 0, HALF)
        add_bias_and_group(0, 1)
        quantise_x_tokens(1, HALF, HALF)
        project_sample(1, 0)
        project_sample(1, 1)
        project_second_half(1)
        transpose_x(2)
        add_bias_and_group(1, 0)
        add_bias_and_group(1, 1)
        group_second_half(0)
        quantise_q(0)
        group_second_half(1)
        quantise_q(1)
        quantise_x(2)
        pair_keys()
        transpose_x(3)
        for i in range(4):
            pass_by_query_token(1, i)
        project(2, (0, 1))

        for i in range(4):
            max_by_query_token(1, i)
            pass_by_key_token(1, i)
            if i < 2:
                project(2, (2 + i,))
        max_by_key_token(1, 0)
        quantise_x(3)
        transpose_x(4)
        project(3, (0, 1))
        max_by_key_token(1, 1)
        max_by_key_token(1, 2)
        project(3, (2, 3))
        regroup(2)

        def last_paired(g):
            for s in range(GROUP):
                if paired(g, s):
                    max_by_query_token_of_pairs(g, s)

        for g in range(2, N_GROUPS):
            when_valid(quantise_x, g + 2)
            quantise_q(g)
            if g == FIRST_PAIRED - 1:
                quantise_pairs()
            when_valid(regroup, g + 1)
            when_valid(transpose_x, g + 3)
            for i in range(4):
                if g > 2 or i == 3:
                    max_by_key_token(g - 1, i)
                if paired(g, i):
                    pass_by_pairs(g, i)
                else:
                    pass_by_query_token(g, i)
            last_paired(g - 1)
            for i in range(4):
                if paired(g, i):
                    max_of_pairs(g, i)
            for i in range(4):
                if not paired(g, i):
                    max_by_query_token(g, i)
                if g + 2 < N_GROUPS:
                    project(g + 2, (i,))
                pass_by_key_token(g, i)
        for i in range(4):
            max_by_key_token(N_GROUPS - 1, i)
        last_paired(N_GROUPS - 1)

        gain = consts.tile([P, 1], F32)
        nc.scalar.activation(out=gain[:], in_=log_gain[:], func=ACT.Exp)
        result = consts.tile([P, N_QUERY, N_KEY], F32)
        last = GROUP * (N_STEPS - 1)
        for first, end in ((0, last), (last, N_QUERY)):
            means = psum_q.tile([P, TOKENS], F32, tag="acc")
            means_of_part = means[:, 0 : N_KEY * (end - first)]
            for maxima in (col_max, row_max):
                nc.tensor.matmul(
                    out=means_of_part,
                    lhsT=mean_weights[:],
                    rhs=maxima[:, first:end, :].rearrange("p a b -> p (a b)"),
                    start=maxima is col_max,
                    stop=maxima is row_max,
                )
            nc.scalar.activation(
                out=result[:, first:end, :].rearrange("p a b -> p (a b)"),
                in_=means_of_part,
                func=ACT.Copy,
                scale=gain[:, 0:1],
            )
        nc.sync.dma_start(out=out.rearrange("a b -> (a b)").unsqueeze(0), in_=result[0:1].rearrange("p a b -> p (a b)"))
